import numpy as np
import ml_dtypes


def mxq(x, axis, fmt="e4m3"):
    dtype, down = {"e4m3": (ml_dtypes.float8_e4m3fn, 7), "e5m2": (ml_dtypes.float8_e5m2, 14)}[fmt]
    v = np.moveaxis(np.asarray(x, np.float32).astype(ml_dtypes.bfloat16).astype(np.float64), axis, -1)
    blocks = v.reshape(v.shape[:-1] + (-1, 32))
    amax = np.abs(blocks).max(-1, keepdims=True)
    byte = np.maximum(np.where(amax > 0, np.frexp(amax)[1] - 1 + 127, 0) - down, 1)
    scale = np.exp2(byte - 127.0)
    codes = (blocks / scale).astype(np.float32).astype(dtype).astype(np.float64)
    return np.moveaxis((codes * scale).reshape(v.shape), -1, axis)


WIDE = False


def mx_kscale(k):
    if not WIDE:
        return np.ones(k)
    levels = np.array([20, -20, 10, -10, 0])
    a = np.random.permutation(np.resize(levels, k // 512 * 4)).reshape(k // 512, 4)
    idx = np.arange(k)
    return np.exp2(a[idx // 512, idx % 128 // 32])


BF16 = ml_dtypes.bfloat16


def bf(x):
    return np.asarray(x, np.float32).astype(BF16)


def f64(x):
    return np.asarray(x).astype(np.float64)


B, S, DIM, H, HD = 4, 128, 128, 16, 128
E = H * HD
T = B * S


def rope_tables():
    inv_freq = 1.0 / (10000.0 ** (np.arange(0, HD, 2) / HD))
    freqs = np.outer(np.arange(S), inv_freq)
    emb = np.concatenate([freqs, freqs], axis=-1)
    return np.cos(emb)[None, None], np.sin(emb)[None, None]


def rotate_half(x):
    x1, x2 = np.split(x, 2, axis=-1)
    return np.concatenate([-x2, x1], axis=-1)


def rotate_half_t(y):
    y1, y2 = np.split(y, 2, axis=-1)
    return np.concatenate([y2, -y1], axis=-1)


def setup_inputs():
    s = mx_kscale(T).reshape(B, S)
    cos, sin = rope_tables()
    query = np.random.standard_normal((B, S, DIM)) * s[:, :, None]
    wq = np.random.standard_normal((E, DIM)) / np.sqrt(DIM)
    bq = np.random.standard_normal(E) * 0.1
    g = np.random.standard_normal((B, H, S, HD)) * np.exp2(np.random.randint(-12, 1, (B, 1, S, 1))) / s[:, None, :, None]
    return {"query": bf(query), "wq": bf(wq), "bq": bf(bq),
            "cos": bf(cos), "sin": bf(sin), "grad_out": bf(g)}


def reference(query, wq, bq, cos, sin, grad_out):
    g = f64(grad_out)
    dq = g * f64(cos) + rotate_half_t(g * f64(sin))
    dp = dq.transpose(0, 2, 1, 3).reshape(T, E)
    x = f64(query).reshape(T, DIM)
    return mxq(dp, 0, "e5m2").T @ mxq(x, 0, "e4m3")

@@ -1,0 +1,127 @@
+from contextlib import ExitStack
+
+import concourse.mybir as mybir
+from concourse.masks import make_identity
+
+BF16 = mybir.dt.bfloat16
+F32 = mybir.dt.float32
+I32 = mybir.dt.int32
+U32 = mybir.dt.uint32
+U8 = mybir.dt.uint8
+E4M3_X4 = mybir.dt.float8_e4m3fn_x4
+E5M2_X4 = mybir.dt.float8_e5m2_x4
+MULT = mybir.AluOpType.mult
+ADD = mybir.AluOpType.add
+
+P = 128
+BATCH, SEQ, DIM, HEADS, HEAD_DIM = 4, 128, 128, 16, 128
+HALF = HEAD_DIM // 2
+PACK = 4
+N_MOVING = 512
+CHUNK_HEADS = 2
+N_CHUNKS = HEADS // CHUNK_HEADS
+
+FLOPS = 2 * BATCH * SEQ * HEADS * HEAD_DIM * DIM
+BYTES = 2 * (BATCH * SEQ * DIM + 2 * SEQ * HEAD_DIM + BATCH * HEADS * SEQ * HEAD_DIM) + 4 * HEADS * HEAD_DIM * DIM
+
+
+def over_heads_and_batches(table):
+    n = table.shape[1]
+    return table.unsqueeze(1).unsqueeze(3).to_broadcast([P, CHUNK_HEADS, n, PACK])
+
+
+def tile_attention_pa_s_kernel(tc, query, wq, bq, cos, sin, grad_out, out):
+    nc = tc.nc
+    with ExitStack() as ctx:
+        const = ctx.enter_context(tc.tile_pool(name="const", bufs=1))
+        const_psum = ctx.enter_context(tc.psum_pool(name="const_psum", bufs=1))
+        loads = ctx.enter_context(tc.tile_pool(name="loads", bufs=N_CHUNKS))
+        work = ctx.enter_context(tc.tile_pool(name="work", bufs=3))
+        acc_psum = ctx.enter_context(tc.psum_pool(name="acc_psum", bufs=4))
+
+        tables = const.tile([P, 2, HEAD_DIM], BF16)
+        sin_raw = const.tile([P, HEAD_DIM], BF16)
+        nc.scalar.dma_start(out=tables[:, 0, :], in_=cos.rearrange("a b s d -> (a b s) d"))
+        nc.scalar.dma_start(out=sin_raw[:], in_=sin.rearrange("a b s d -> (a b s) d"))
+        nc.vector.tensor_copy(out=tables[:, 1, 0:HALF], in_=sin_raw[:, HALF:HEAD_DIM])
+        nc.vector.tensor_scalar_mul(out=tables[:, 1, HALF:HEAD_DIM], in0=sin_raw[:, 0:HALF], scalar1=-1.0)
+        identity = const.tile([P, P], BF16)
+        make_identity(nc, identity[:])
+        tables_psum = const_psum.tile([P, 2, HEAD_DIM], F32)
+        nc.tensor.matmul(
+            out=tables_psum[:].rearrange("p t d -> p (t d)"),
+            lhsT=identity[:],
+            rhs=tables[:].rearrange("p t d -> p (t d)"),
+            start=True,
+            stop=True,
+        )
+
+        x_raw = const.tile([P, BATCH, DIM], BF16)
+        nc.scalar.dma_start(out=x_raw[:], in_=query.rearrange("b s i -> s b i"))
+        x_grouped = const.tile([P, DIM, PACK], BF16, align_bytes=64)
+        nc.vector.tensor_copy(out=x_grouped[:], in_=x_raw[:].rearrange("p b i -> p i b"))
+        x_codes = const.tile([P, N_MOVING], U32, align_bytes=64)
+        x_scales = const.tile([P, N_MOVING], U8, align_bytes=64)
+        nc.vector.memset(x_codes[:, DIM:N_MOVING].bitcast(I32), 0)
+        nc.vector.memset(x_scales[:, DIM:N_MOVING].bitcast(I32), 0)
+        nc.vector.quantize_mx(
+            out=x_codes[:, 0:DIM].bitcast(E4M3_X4),
+            scales=x_scales[:, 0:DIM],
+            in_=x_grouped[:].rearrange("p i b -> p (i b)"),
+        )
+
+        dp_codes = const.tile([P, HEADS * HEAD_DIM], U32, align_bytes=64)
+        dp_scales = const.tile([P, HEADS * HEAD_DIM], U8, align_bytes=64)
+        out_by_head = out.rearrange("(h d) i -> d h i", d=HEAD_DIM)
+
+        for c in range(N_CHUNKS):
+            heads = slice(c * CHUNK_HEADS, (c + 1) * CHUNK_HEADS)
+            first_column = c * CHUNK_HEADS * HEAD_DIM
+            columns = slice(first_column, first_column + CHUNK_HEADS * HEAD_DIM)
+
+            g = loads.tile([P, BATCH, CHUNK_HEADS, HEAD_DIM], BF16)
+            for b in range(BATCH):
+                nc.sync.dma_start(out=g[:, b], in_=grad_out[b, heads].rearrange("h s d -> s h d"))
+
+            g_words = g[:].rearrange("p b h d -> p h d b")
+            g_cos = work.tile([P, CHUNK_HEADS, HEAD_DIM, PACK], F32)
+            g_sin = work.tile([P, CHUNK_HEADS, HEAD_DIM, PACK], F32)
+            nc.vector.tensor_tensor(
+                out=g_cos[:], in0=g_words, in1=over_heads_and_batches(tables_psum[:, 0, :]), op=MULT
+            )
+            nc.vector.tensor_tensor(
+                out=g_sin[:, :, 0:HALF, :],
+                in0=g_words[:, :, HALF:HEAD_DIM, :],
+                in1=over_heads_and_batches(tables_psum[:, 1, 0:HALF]),
+                op=MULT,
+            )
+            nc.vector.tensor_tensor(
+                out=g_sin[:, :, HALF:HEAD_DIM, :],
+                in0=g_words[:, :, 0:HALF, :],
+                in1=over_heads_and_batches(tables_psum[:, 1, HALF:HEAD_DIM]),
+                op=MULT,
+            )
+            dq = work.tile([P, CHUNK_HEADS, HEAD_DIM, PACK], BF16, align_bytes=64)
+            nc.gpsimd.tensor_tensor(out=dq[:], in0=g_cos[:], in1=g_sin[:], op=ADD)
+
+            nc.vector.quantize_mx(
+                out=dp_codes[:, columns].bitcast(E5M2_X4),
+                scales=dp_scales[:, columns],
+                in_=dq[:].rearrange("p h d b -> p (h d b)"),
+            )
+
+            result = work.tile([P, CHUNK_HEADS, DIM], F32)
+            for k in range(CHUNK_HEADS):
+                head_columns = slice(first_column + k * HEAD_DIM, first_column + (k + 1) * HEAD_DIM)
+                acc = acc_psum.tile([P, N_MOVING], F32)
+                nc.tensor.matmul_mx(
+                    out=acc[:],
+                    lhsT=dp_codes[:, head_columns].bitcast(E5M2_X4),
+                    lhsT_scale=dp_scales[:, head_columns],
+                    rhs=x_codes[:].bitcast(E4M3_X4),
+                    rhs_scale=x_scales[:],
+                    start=True,
+                    stop=True,
+                )
+                nc.scalar.copy(out=result[:, k, :], in_=acc[:, 0:DIM])
+            nc.sync.dma_start(out=out_by_head[:, heads, :], in_=result[:])

@@ -20,6 +20,7 @@ PACK = 4
 N_MOVING = 512
 CHUNK_HEADS = 2
 N_CHUNKS = HEADS // CHUNK_HEADS
+AHEAD = 2
 
 FLOPS = 2 * BATCH * SEQ * HEADS * HEAD_DIM * DIM
 BYTES = 2 * (BATCH * SEQ * DIM + 2 * SEQ * HEAD_DIM + BATCH * HEADS * SEQ * HEAD_DIM) + 4 * HEADS * HEAD_DIM * DIM
@@ -36,17 +37,30 @@ def tile_attention_pa_s_kernel(tc, query, wq, bq, cos, sin, grad_out, out):
         const = ctx.enter_context(tc.tile_pool(name="const", bufs=1))
         const_psum = ctx.enter_context(tc.psum_pool(name="const_psum", bufs=1))
         loads = ctx.enter_context(tc.tile_pool(name="loads", bufs=N_CHUNKS))
-        work = ctx.enter_context(tc.tile_pool(name="work", bufs=3))
+        work = ctx.enter_context(tc.tile_pool(name="work", bufs=AHEAD + 2))
         acc_psum = ctx.enter_context(tc.psum_pool(name="acc_psum", bufs=4))
+        ctx.enter_context(tc.manual_schedule())
 
         tables = const.tile([P, 2, HEAD_DIM], BF16)
         sin_raw = const.tile([P, HEAD_DIM], BF16)
+        x_raw = const.tile([P, BATCH, DIM], BF16)
         nc.scalar.dma_start(out=tables[:, 0, :], in_=cos.rearrange("a b s d -> (a b s) d"))
         nc.scalar.dma_start(out=sin_raw[:], in_=sin.rearrange("a b s d -> (a b s) d"))
-        nc.vector.tensor_copy(out=tables[:, 1, 0:HALF], in_=sin_raw[:, HALF:HEAD_DIM])
-        nc.vector.tensor_scalar_mul(out=tables[:, 1, HALF:HEAD_DIM], in0=sin_raw[:, 0:HALF], scalar1=-1.0)
+        nc.scalar.dma_start(out=x_raw[:], in_=query.rearrange("b s i -> s b i"))
+        g_of_chunk = []
+        for c in range(N_CHUNKS):
+            g = loads.tile([P, BATCH, CHUNK_HEADS, HEAD_DIM], BF16)
+            for b in range(BATCH):
+                nc.sync.dma_start(
+                    out=g[:, b],
+                    in_=grad_out[b, c * CHUNK_HEADS : (c + 1) * CHUNK_HEADS].rearrange("h s d -> s h d"),
+                )
+            g_of_chunk.append(g)
+
         identity = const.tile([P, P], BF16)
         make_identity(nc, identity[:])
+        nc.vector.tensor_copy(out=tables[:, 1, 0:HALF], in_=sin_raw[:, HALF:HEAD_DIM])
+        nc.vector.tensor_scalar_mul(out=tables[:, 1, HALF:HEAD_DIM], in0=sin_raw[:, 0:HALF], scalar1=-1.0)
         tables_psum = const_psum.tile([P, 2, HEAD_DIM], F32)
         nc.tensor.matmul(
             out=tables_psum[:].rearrange("p t d -> p (t d)"),
@@ -56,63 +70,67 @@ def tile_attention_pa_s_kernel(tc, query, wq, bq, cos, sin, grad_out, out):
             stop=True,
         )
 
-        x_raw = const.tile([P, BATCH, DIM], BF16)
-        nc.scalar.dma_start(out=x_raw[:], in_=query.rearrange("b s i -> s b i"))
-        x_grouped = const.tile([P, DIM, PACK], BF16, align_bytes=64)
-        nc.vector.tensor_copy(out=x_grouped[:], in_=x_raw[:].rearrange("p b i -> p i b"))
         x_codes = const.tile([P, N_MOVING], U32, align_bytes=64)
         x_scales = const.tile([P, N_MOVING], U8, align_bytes=64)
-        nc.vector.memset(x_codes[:, DIM:N_MOVING].bitcast(I32), 0)
-        nc.vector.memset(x_scales[:, DIM:N_MOVING].bitcast(I32), 0)
-        nc.vector.quantize_mx(
-            out=x_codes[:, 0:DIM].bitcast(E4M3_X4),
-            scales=x_scales[:, 0:DIM],
-            in_=x_grouped[:].rearrange("p i b -> p (i b)"),
-        )
-
         dp_codes = const.tile([P, HEADS * HEAD_DIM], U32, align_bytes=64)
         dp_scales = const.tile([P, HEADS * HEAD_DIM], U8, align_bytes=64)
         out_by_head = out.rearrange("(h d) i -> d h i", d=HEAD_DIM)
+        products_of_chunk = []
+        dq_of_chunk = []
 
-        for c in range(N_CHUNKS):
-            heads = slice(c * CHUNK_HEADS, (c + 1) * CHUNK_HEADS)
-            first_column = c * CHUNK_HEADS * HEAD_DIM
-            columns = slice(first_column, first_column + CHUNK_HEADS * HEAD_DIM)
+        def quantise_x():
+            x_grouped = const.tile([P, DIM, PACK], BF16, align_bytes=64)
+            nc.vector.tensor_copy(out=x_grouped[:], in_=x_raw[:].rearrange("p b i -> p i b"))
+            nc.vector.memset(x_codes[:, DIM:N_MOVING].bitcast(I32), 0)
+            nc.vector.memset(x_scales[:, DIM:N_MOVING].bitcast(I32), 0)
+            nc.vector.quantize_mx(
+                out=x_codes[:, 0:DIM].bitcast(E4M3_X4),
+                scales=x_scales[:, 0:DIM],
+                in_=x_grouped[:].rearrange("p i b -> p (i b)"),
+            )
 
-            g = loads.tile([P, BATCH, CHUNK_HEADS, HEAD_DIM], BF16)
-            for b in range(BATCH):
-                nc.sync.dma_start(out=g[:, b], in_=grad_out[b, heads].rearrange("h s d -> s h d"))
-
-            g_words = g[:].rearrange("p b h d -> p h d b")
+        def products(c):
+            table_source = tables if c == 0 else tables_psum
+            g_words = g_of_chunk[c][:].rearrange("p b h d -> p h d b")
             g_cos = work.tile([P, CHUNK_HEADS, HEAD_DIM, PACK], F32)
             g_sin = work.tile([P, CHUNK_HEADS, HEAD_DIM, PACK], F32)
             nc.vector.tensor_tensor(
-                out=g_cos[:], in0=g_words, in1=over_heads_and_batches(tables_psum[:, 0, :]), op=MULT
+                out=g_cos[:], in0=g_words, in1=over_heads_and_batches(table_source[:, 0, :]), op=MULT
             )
             nc.vector.tensor_tensor(
                 out=g_sin[:, :, 0:HALF, :],
                 in0=g_words[:, :, HALF:HEAD_DIM, :],
-                in1=over_heads_and_batches(tables_psum[:, 1, 0:HALF]),
+                in1=over_heads_and_batches(table_source[:, 1, 0:HALF]),
                 op=MULT,
             )
             nc.vector.tensor_tensor(
                 out=g_sin[:, :, HALF:HEAD_DIM, :],
                 in0=g_words[:, :, 0:HALF, :],
-                in1=over_heads_and_batches(tables_psum[:, 1, HALF:HEAD_DIM]),
+                in1=over_heads_and_batches(table_source[:, 1, HALF:HEAD_DIM]),
                 op=MULT,
             )
-            dq = work.tile([P, CHUNK_HEADS, HEAD_DIM, PACK], BF16, align_bytes=64)
-            nc.gpsimd.tensor_tensor(out=dq[:], in0=g_cos[:], in1=g_sin[:], op=ADD)
+            products_of_chunk.append((g_cos, g_sin))
 
+        def add(c):
+            g_cos, g_sin = products_of_chunk[c]
+            dq = work.tile([P, CHUNK_HEADS, HEAD_DIM, PACK], BF16, align_bytes=64)
+            engine = nc.vector if c == N_CHUNKS - 1 else nc.gpsimd
+            engine.tensor_tensor(out=dq[:], in0=g_cos[:], in1=g_sin[:], op=ADD)
+            dq_of_chunk.append(dq)
+
+        def quantise(c):
+            columns = slice(c * CHUNK_HEADS * HEAD_DIM, (c + 1) * CHUNK_HEADS * HEAD_DIM)
             nc.vector.quantize_mx(
                 out=dp_codes[:, columns].bitcast(E5M2_X4),
                 scales=dp_scales[:, columns],
-                in_=dq[:].rearrange("p h d b -> p (h d b)"),
+                in_=dq_of_chunk[c][:].rearrange("p h d b -> p (h d b)"),
             )
 
+        def multiply_and_store(c):
             result = work.tile([P, CHUNK_HEADS, DIM], F32)
             for k in range(CHUNK_HEADS):
-                head_columns = slice(first_column + k * HEAD_DIM, first_column + (k + 1) * HEAD_DIM)
+                h = c * CHUNK_HEADS + k
+                head_columns = slice(h * HEAD_DIM, (h + 1) * HEAD_DIM)
                 acc = acc_psum.tile([P, N_MOVING], F32)
                 nc.tensor.matmul_mx(
                     out=acc[:],
@@ -124,4 +142,14 @@ def tile_attention_pa_s_kernel(tc, query, wq, bq, cos, sin, grad_out, out):
                     stop=True,
                 )
                 nc.scalar.copy(out=result[:, k, :], in_=acc[:, 0:DIM])
-            nc.sync.dma_start(out=out_by_head[:, heads, :], in_=result[:])
+            nc.sync.dma_start(out=out_by_head[:, c * CHUNK_HEADS : (c + 1) * CHUNK_HEADS, :], in_=result[:])
+
+        for c in range(AHEAD):
+            products(c)
+        quantise_x()
+        for c in range(N_CHUNKS):
+            add(c)
+            if c + AHEAD < N_CHUNKS:
+                products(c + AHEAD)
+            quantise(c)
+            multiply_and_store(c)

@@ -20,7 +20,6 @@ PACK = 4
 N_MOVING = 512
 CHUNK_HEADS = 2
 N_CHUNKS = HEADS // CHUNK_HEADS
-AHEAD = 2
 
 FLOPS = 2 * BATCH * SEQ * HEADS * HEAD_DIM * DIM
 BYTES = 2 * (BATCH * SEQ * DIM + 2 * SEQ * HEAD_DIM + BATCH * HEADS * SEQ * HEAD_DIM) + 4 * HEADS * HEAD_DIM * DIM
@@ -37,16 +36,23 @@ def tile_attention_pa_s_kernel(tc, query, wq, bq, cos, sin, grad_out, out):
         const = ctx.enter_context(tc.tile_pool(name="const", bufs=1))
         const_psum = ctx.enter_context(tc.psum_pool(name="const_psum", bufs=1))
         loads = ctx.enter_context(tc.tile_pool(name="loads", bufs=N_CHUNKS))
-        work = ctx.enter_context(tc.tile_pool(name="work", bufs=AHEAD + 2))
+        work = ctx.enter_context(tc.tile_pool(name="work", bufs=3))
+        handover = ctx.enter_context(tc.tile_pool(name="handover", bufs=1))
         acc_psum = ctx.enter_context(tc.psum_pool(name="acc_psum", bufs=4))
         ctx.enter_context(tc.manual_schedule())
+
+        x_codes = const.tile([P, N_MOVING], U32, align_bytes=64)
+        x_scales = const.tile([P, N_MOVING], U8, align_bytes=64)
+        dp_codes = const.tile([P, HEADS * HEAD_DIM], U32, align_bytes=64)
+        dp_scales = const.tile([P, HEADS * HEAD_DIM], U8, align_bytes=64)
+        nc.vector.memset(x_codes[:, DIM:N_MOVING].bitcast(I32), 0)
+        nc.vector.memset(x_scales[:, DIM:N_MOVING].bitcast(I32), 0)
 
         tables = const.tile([P, 2, HEAD_DIM], BF16)
         sin_raw = const.tile([P, HEAD_DIM], BF16)
         x_raw = const.tile([P, BATCH, DIM], BF16)
         nc.scalar.dma_start(out=tables[:, 0, :], in_=cos.rearrange("a b s d -> (a b s) d"))
         nc.scalar.dma_start(out=sin_raw[:], in_=sin.rearrange("a b s d -> (a b s) d"))
-        nc.scalar.dma_start(out=x_raw[:], in_=query.rearrange("b s i -> s b i"))
         g_of_chunk = []
         for c in range(N_CHUNKS):
             g = loads.tile([P, BATCH, CHUNK_HEADS, HEAD_DIM], BF16)
@@ -56,6 +62,8 @@ def tile_attention_pa_s_kernel(tc, query, wq, bq, cos, sin, grad_out, out):
                     in_=grad_out[b, c * CHUNK_HEADS : (c + 1) * CHUNK_HEADS].rearrange("h s d -> s h d"),
                 )
             g_of_chunk.append(g)
+            if c == 1:
+                nc.sync.dma_start(out=x_raw[:], in_=query.rearrange("b s i -> s b i"))
 
         identity = const.tile([P, P], BF16)
         make_identity(nc, identity[:])
@@ -70,19 +78,13 @@ def tile_attention_pa_s_kernel(tc, query, wq, bq, cos, sin, grad_out, out):
             stop=True,
         )
 
-        x_codes = const.tile([P, N_MOVING], U32, align_bytes=64)
-        x_scales = const.tile([P, N_MOVING], U8, align_bytes=64)
-        dp_codes = const.tile([P, HEADS * HEAD_DIM], U32, align_bytes=64)
-        dp_scales = const.tile([P, HEADS * HEAD_DIM], U8, align_bytes=64)
         out_by_head = out.rearrange("(h d) i -> d h i", d=HEAD_DIM)
         products_of_chunk = []
         dq_of_chunk = []
 
         def quantise_x():
             x_grouped = const.tile([P, DIM, PACK], BF16, align_bytes=64)
-            nc.vector.tensor_copy(out=x_grouped[:], in_=x_raw[:].rearrange("p b i -> p i b"))
-            nc.vector.memset(x_codes[:, DIM:N_MOVING].bitcast(I32), 0)
-            nc.vector.memset(x_scales[:, DIM:N_MOVING].bitcast(I32), 0)
+            nc.scalar.copy(out=x_grouped[:], in_=x_raw[:].rearrange("p b i -> p i b"))
             nc.vector.quantize_mx(
                 out=x_codes[:, 0:DIM].bitcast(E4M3_X4),
                 scales=x_scales[:, 0:DIM],
@@ -113,7 +115,7 @@ def tile_attention_pa_s_kernel(tc, query, wq, bq, cos, sin, grad_out, out):
 
         def add(c):
             g_cos, g_sin = products_of_chunk[c]
-            dq = work.tile([P, CHUNK_HEADS, HEAD_DIM, PACK], BF16, align_bytes=64)
+            dq = handover.tile([P, CHUNK_HEADS, HEAD_DIM, PACK], BF16, align_bytes=64)
             engine = nc.vector if c == N_CHUNKS - 1 else nc.gpsimd
             engine.tensor_tensor(out=dq[:], in0=g_cos[:], in1=g_sin[:], op=ADD)
             dq_of_chunk.append(dq)
@@ -144,12 +146,12 @@ def tile_attention_pa_s_kernel(tc, query, wq, bq, cos, sin, grad_out, out):
                 nc.scalar.copy(out=result[:, k, :], in_=acc[:, 0:DIM])
             nc.sync.dma_start(out=out_by_head[:, c * CHUNK_HEADS : (c + 1) * CHUNK_HEADS, :], in_=result[:])
 
-        for c in range(AHEAD):
-            products(c)
-        quantise_x()
+        products(0)
         for c in range(N_CHUNKS):
             add(c)
-            if c + AHEAD < N_CHUNKS:
-                products(c + AHEAD)
+            if c + 1 < N_CHUNKS:
+                products(c + 1)
+            if c == 0:
+                quantise_x()
             quantise(c)
             multiply_and_store(c)

@@ -38,6 +38,7 @@ def tile_attention_pa_s_kernel(tc, query, wq, bq, cos, sin, grad_out, out):
         loads = ctx.enter_context(tc.tile_pool(name="loads", bufs=N_CHUNKS))
         work = ctx.enter_context(tc.tile_pool(name="work", bufs=3))
         handover = ctx.enter_context(tc.tile_pool(name="handover", bufs=1))
+        results = ctx.enter_context(tc.tile_pool(name="results", bufs=2))
         acc_psum = ctx.enter_context(tc.psum_pool(name="acc_psum", bufs=4))
         ctx.enter_context(tc.manual_schedule())
 
@@ -80,7 +81,6 @@ def tile_attention_pa_s_kernel(tc, query, wq, bq, cos, sin, grad_out, out):
 
         out_by_head = out.rearrange("(h d) i -> d h i", d=HEAD_DIM)
         products_of_chunk = []
-        dq_of_chunk = []
 
         def quantise_x():
             x_grouped = const.tile([P, DIM, PACK], BF16, align_bytes=64)
@@ -113,26 +113,23 @@ def tile_attention_pa_s_kernel(tc, query, wq, bq, cos, sin, grad_out, out):
             )
             products_of_chunk.append((g_cos, g_sin))
 
-        def add(c):
+        def add(c, dq_chunk):
             g_cos, g_sin = products_of_chunk[c]
-            dq = handover.tile([P, CHUNK_HEADS, HEAD_DIM, PACK], BF16, align_bytes=64)
             engine = nc.vector if c == N_CHUNKS - 1 else nc.gpsimd
-            engine.tensor_tensor(out=dq[:], in0=g_cos[:], in1=g_sin[:], op=ADD)
-            dq_of_chunk.append(dq)
+            engine.tensor_tensor(out=dq_chunk, in0=g_cos[:], in1=g_sin[:], op=ADD)
 
-        def quantise(c):
-            columns = slice(c * CHUNK_HEADS * HEAD_DIM, (c + 1) * CHUNK_HEADS * HEAD_DIM)
+        def quantise(first_head, n_heads, dq):
+            columns = slice(first_head * HEAD_DIM, (first_head + n_heads) * HEAD_DIM)
             nc.vector.quantize_mx(
                 out=dp_codes[:, columns].bitcast(E5M2_X4),
                 scales=dp_scales[:, columns],
-                in_=dq_of_chunk[c][:].rearrange("p h d b -> p (h d b)"),
+                in_=dq[:].rearrange("p h d b -> p (h d b)"),
             )
 
-        def multiply_and_store(c):
-            result = work.tile([P, CHUNK_HEADS, DIM], F32)
-            for k in range(CHUNK_HEADS):
-                h = c * CHUNK_HEADS + k
-                head_columns = slice(h * HEAD_DIM, (h + 1) * HEAD_DIM)
+        def multiply_and_store(first_head, n_heads):
+            result = results.tile([P, n_heads, DIM], F32, tag="result")
+            for k in range(n_heads):
+                head_columns = slice((first_head + k) * HEAD_DIM, (first_head + k + 1) * HEAD_DIM)
                 acc = acc_psum.tile([P, N_MOVING], F32)
                 nc.tensor.matmul_mx(
                     out=acc[:],
@@ -144,14 +141,20 @@ def tile_attention_pa_s_kernel(tc, query, wq, bq, cos, sin, grad_out, out):
                     stop=True,
                 )
                 nc.scalar.copy(out=result[:, k, :], in_=acc[:, 0:DIM])
-            nc.sync.dma_start(out=out_by_head[:, c * CHUNK_HEADS : (c + 1) * CHUNK_HEADS, :], in_=result[:])
+            nc.sync.dma_start(out=out_by_head[:, first_head : first_head + n_heads, :], in_=result[:])
 
         products(0)
-        for c in range(N_CHUNKS):
-            add(c)
-            if c + 1 < N_CHUNKS:
-                products(c + 1)
-            if c == 0:
+        first_chunk = 0
+        while first_chunk < N_CHUNKS:
+            n_chunks = max(1, (N_CHUNKS - first_chunk) // 2)
+            dq = handover.tile([P, n_chunks * CHUNK_HEADS, HEAD_DIM, PACK], BF16, tag="dq", align_bytes=64)
+            for k in range(n_chunks):
+                c = first_chunk + k
+                add(c, dq[:, k * CHUNK_HEADS : (k + 1) * CHUNK_HEADS])
+                if c + 1 < N_CHUNKS:
+                    products(c + 1)
+            if first_chunk == 0:
                 quantise_x()
-            quantise(c)
-            multiply_and_store(c)
+            quantise(first_chunk * CHUNK_HEADS, n_chunks * CHUNK_HEADS, dq)
+            multiply_and_store(first_chunk * CHUNK_HEADS, n_chunks * CHUNK_HEADS)
+            first_chunk += n_chunks

@@ -1,7 +1,6 @@
 from contextlib import ExitStack
 
 import concourse.mybir as mybir
-from concourse.masks import make_identity
 
 BF16 = mybir.dt.bfloat16
 F32 = mybir.dt.float32
@@ -12,34 +11,32 @@ E4M3_X4 = mybir.dt.float8_e4m3fn_x4
 E5M2_X4 = mybir.dt.float8_e5m2_x4
 MULT = mybir.AluOpType.mult
 ADD = mybir.AluOpType.add
+COPY = mybir.ActivationFunctionType.Copy
 
 P = 128
 BATCH, SEQ, DIM, HEADS, HEAD_DIM = 4, 128, 128, 16, 128
 HALF = HEAD_DIM // 2
 PACK = 4
 N_MOVING = 512
-CHUNK_HEADS = 2
+CHUNK_HEADS = 4
 N_CHUNKS = HEADS // CHUNK_HEADS
+WINDOW = 8
+N_WINDOWS = HEAD_DIM // WINDOW
+GROUP = 16
+Q_LAG = 2
+SPLIT = 84
+STORE_WINDOWS = 4
 
 FLOPS = 2 * BATCH * SEQ * HEADS * HEAD_DIM * DIM
 BYTES = 2 * (BATCH * SEQ * DIM + 2 * SEQ * HEAD_DIM + BATCH * HEADS * SEQ * HEAD_DIM) + 4 * HEADS * HEAD_DIM * DIM
-
-
-def over_heads_and_batches(table):
-    n = table.shape[1]
-    return table.unsqueeze(1).unsqueeze(3).to_broadcast([P, CHUNK_HEADS, n, PACK])
 
 
 def tile_attention_pa_s_kernel(tc, query, wq, bq, cos, sin, grad_out, out):
     nc = tc.nc
     with ExitStack() as ctx:
         const = ctx.enter_context(tc.tile_pool(name="const", bufs=1))
-        const_psum = ctx.enter_context(tc.psum_pool(name="const_psum", bufs=1))
         loads = ctx.enter_context(tc.tile_pool(name="loads", bufs=N_CHUNKS))
-        work = ctx.enter_context(tc.tile_pool(name="work", bufs=3))
-        handover = ctx.enter_context(tc.tile_pool(name="handover", bufs=1))
-        results = ctx.enter_context(tc.tile_pool(name="results", bufs=2))
-        acc_psum = ctx.enter_context(tc.psum_pool(name="acc_psum", bufs=4))
+        acc_psum = ctx.enter_context(tc.psum_pool(name="acc_psum", bufs=6))
         ctx.enter_context(tc.manual_schedule())
 
         x_codes = const.tile([P, N_MOVING], U32, align_bytes=64)
@@ -49,10 +46,10 @@ def tile_attention_pa_s_kernel(tc, query, wq, bq, cos, sin, grad_out, out):
         nc.vector.memset(x_codes[:, DIM:N_MOVING].bitcast(I32), 0)
         nc.vector.memset(x_scales[:, DIM:N_MOVING].bitcast(I32), 0)
 
-        tables = const.tile([P, 2, HEAD_DIM], BF16)
+        cos_raw = const.tile([P, HEAD_DIM], BF16)
         sin_raw = const.tile([P, HEAD_DIM], BF16)
         x_raw = const.tile([P, BATCH, DIM], BF16)
-        nc.scalar.dma_start(out=tables[:, 0, :], in_=cos.rearrange("a b s d -> (a b s) d"))
+        nc.scalar.dma_start(out=cos_raw[:], in_=cos.rearrange("a b s d -> (a b s) d"))
         nc.scalar.dma_start(out=sin_raw[:], in_=sin.rearrange("a b s d -> (a b s) d"))
         g_of_chunk = []
         for c in range(N_CHUNKS):
@@ -63,98 +60,87 @@ def tile_attention_pa_s_kernel(tc, query, wq, bq, cos, sin, grad_out, out):
                     in_=grad_out[b, c * CHUNK_HEADS : (c + 1) * CHUNK_HEADS].rearrange("h s d -> s h d"),
                 )
             g_of_chunk.append(g)
-            if c == 1:
+            if c == 0:
                 nc.sync.dma_start(out=x_raw[:], in_=query.rearrange("b s i -> s b i"))
 
-        identity = const.tile([P, P], BF16)
-        make_identity(nc, identity[:])
-        nc.vector.tensor_copy(out=tables[:, 1, 0:HALF], in_=sin_raw[:, HALF:HEAD_DIM])
-        nc.vector.tensor_scalar_mul(out=tables[:, 1, HALF:HEAD_DIM], in0=sin_raw[:, 0:HALF], scalar1=-1.0)
-        tables_psum = const_psum.tile([P, 2, HEAD_DIM], F32)
-        nc.tensor.matmul(
-            out=tables_psum[:].rearrange("p t d -> p (t d)"),
-            lhsT=identity[:],
-            rhs=tables[:].rearrange("p t d -> p (t d)"),
-            start=True,
-            stop=True,
-        )
+        cos32 = const.tile([P, HEAD_DIM], F32)
+        sinr32 = const.tile([P, HEAD_DIM], F32)
+        nc.vector.tensor_copy(out=cos32[:], in_=cos_raw[:])
+        nc.vector.tensor_copy(out=sinr32[:, 0:HALF], in_=sin_raw[:, HALF:HEAD_DIM])
+        nc.vector.tensor_scalar_mul(out=sinr32[:, HALF:HEAD_DIM], in0=sin_raw[:, 0:HALF], scalar1=-1.0)
 
-        out_by_head = out.rearrange("(h d) i -> d h i", d=HEAD_DIM)
-        products_of_chunk = []
-
-        def quantise_x():
-            x_grouped = const.tile([P, DIM, PACK], BF16, align_bytes=64)
-            nc.scalar.copy(out=x_grouped[:], in_=x_raw[:].rearrange("p b i -> p i b"))
-            nc.vector.quantize_mx(
-                out=x_codes[:, 0:DIM].bitcast(E4M3_X4),
-                scales=x_scales[:, 0:DIM],
-                in_=x_grouped[:].rearrange("p i b -> p (i b)"),
-            )
-
-        def products(c):
-            table_source = tables if c == 0 else tables_psum
+        g_il = const.tile([P, HEADS, HEAD_DIM, PACK], BF16)
+        x_grouped = const.tile([P, DIM, PACK], BF16, align_bytes=64)
+        for c in range(N_CHUNKS):
+            heads = slice(c * CHUNK_HEADS, (c + 1) * CHUNK_HEADS)
             g_words = g_of_chunk[c][:].rearrange("p b h d -> p h d b")
-            g_cos = work.tile([P, CHUNK_HEADS, HEAD_DIM, PACK], F32)
-            g_sin = work.tile([P, CHUNK_HEADS, HEAD_DIM, PACK], F32)
-            nc.vector.tensor_tensor(
-                out=g_cos[:], in0=g_words, in1=over_heads_and_batches(table_source[:, 0, :]), op=MULT
-            )
-            nc.vector.tensor_tensor(
-                out=g_sin[:, :, 0:HALF, :],
-                in0=g_words[:, :, HALF:HEAD_DIM, :],
-                in1=over_heads_and_batches(table_source[:, 1, 0:HALF]),
-                op=MULT,
-            )
-            nc.vector.tensor_tensor(
-                out=g_sin[:, :, HALF:HEAD_DIM, :],
-                in0=g_words[:, :, 0:HALF, :],
-                in1=over_heads_and_batches(table_source[:, 1, HALF:HEAD_DIM]),
-                op=MULT,
-            )
-            products_of_chunk.append((g_cos, g_sin))
+            nc.vector.tensor_copy(out=g_il[:, heads, 0:SPLIT, :], in_=g_words[:, :, 0:SPLIT, :])
+            nc.scalar.copy(out=g_il[:, heads, SPLIT:HEAD_DIM, :], in_=g_words[:, :, SPLIT:HEAD_DIM, :])
+            if c == 0:
+                nc.scalar.copy(out=x_grouped[:], in_=x_raw[:].rearrange("p b i -> p i b"))
+            if c == 1:
+                nc.vector.quantize_mx(
+                    out=x_codes[:, 0:DIM].bitcast(E4M3_X4),
+                    scales=x_scales[:, 0:DIM],
+                    in_=x_grouped[:].rearrange("p i b -> p (i b)"),
+                )
 
-        def add(c, dq_chunk):
-            g_cos, g_sin = products_of_chunk[c]
-            engine = nc.vector if c == N_CHUNKS - 1 else nc.gpsimd
-            engine.tensor_tensor(out=dq_chunk, in0=g_cos[:], in1=g_sin[:], op=ADD)
+        g_cos = const.tile([P, HEAD_DIM, HEADS, PACK], F32)
+        dq = const.tile([P, HEAD_DIM, HEADS, PACK], BF16, align_bytes=64)
+        result = const.tile([P, N_WINDOWS, DIM], F32)
+        out_view = out.rearrange("(h dl j) i -> dl h j i", h=HEADS, dl=WINDOW, j=N_WINDOWS)
+        acc_of_window = {}
 
-        def quantise(first_head, n_heads, dq):
-            columns = slice(first_head * HEAD_DIM, (first_head + n_heads) * HEAD_DIM)
+        def quantise_and_multiply(q):
+            slots = slice(q * GROUP, (q + 1) * GROUP)
+            columns = slice(q * GROUP * HEADS, (q + 1) * GROUP * HEADS)
             nc.vector.quantize_mx(
                 out=dp_codes[:, columns].bitcast(E5M2_X4),
                 scales=dp_scales[:, columns],
-                in_=dq[:].rearrange("p h d b -> p (h d b)"),
+                in_=dq[:, slots].rearrange("p s h b -> p (s h b)"),
             )
-
-        def multiply_and_store(first_head, n_heads):
-            result = results.tile([P, n_heads, DIM], F32, tag="result")
-            for k in range(n_heads):
-                head_columns = slice((first_head + k) * HEAD_DIM, (first_head + k + 1) * HEAD_DIM)
+            for j in range(q * GROUP // WINDOW, (q + 1) * GROUP // WINDOW):
+                window_columns = slice(j * P, (j + 1) * P)
                 acc = acc_psum.tile([P, N_MOVING], F32)
                 nc.tensor.matmul_mx(
                     out=acc[:],
-                    lhsT=dp_codes[:, head_columns].bitcast(E5M2_X4),
-                    lhsT_scale=dp_scales[:, head_columns],
+                    lhsT=dp_codes[:, window_columns].bitcast(E5M2_X4),
+                    lhsT_scale=dp_scales[:, window_columns],
                     rhs=x_codes[:].bitcast(E4M3_X4),
                     rhs_scale=x_scales[:],
                     start=True,
                     stop=True,
                 )
-                nc.scalar.copy(out=result[:, k, :], in_=acc[:, 0:DIM])
-            nc.sync.dma_start(out=out_by_head[:, first_head : first_head + n_heads, :], in_=result[:])
+                acc_of_window[j] = acc
 
-        products(0)
-        first_chunk = 0
-        while first_chunk < N_CHUNKS:
-            n_chunks = max(1, (N_CHUNKS - first_chunk) // 2)
-            dq = handover.tile([P, n_chunks * CHUNK_HEADS, HEAD_DIM, PACK], BF16, tag="dq", align_bytes=64)
-            for k in range(n_chunks):
-                c = first_chunk + k
-                add(c, dq[:, k * CHUNK_HEADS : (k + 1) * CHUNK_HEADS])
-                if c + 1 < N_CHUNKS:
-                    products(c + 1)
-            if first_chunk == 0:
-                quantise_x()
-            quantise(first_chunk * CHUNK_HEADS, n_chunks * CHUNK_HEADS, dq)
-            multiply_and_store(first_chunk * CHUNK_HEADS, n_chunks * CHUNK_HEADS)
-            first_chunk += n_chunks
+        def empty_and_store(q):
+            for j in range(q * GROUP // WINDOW, (q + 1) * GROUP // WINDOW):
+                nc.scalar.copy(out=result[:, j, :], in_=acc_of_window[j][:, 0:DIM])
+                if (j + 1) % STORE_WINDOWS == 0:
+                    windows = slice(j + 1 - STORE_WINDOWS, j + 1)
+                    for dl in range(WINDOW):
+                        rows = slice(dl * HEADS, (dl + 1) * HEADS)
+                        nc.sync.dma_start(out=out_view[dl, :, windows, :], in_=result[rows, windows, :])
+
+        n_groups = HEAD_DIM // GROUP
+        for slot in range(HEAD_DIM):
+            j, dl = slot // WINDOW, slot % WINDOW
+            d = N_WINDOWS * dl + j
+            partner = d + HALF if d < HALF else d - HALF
+            nc.scalar.activation(out=g_cos[:, slot], in_=g_il[:, :, d, :], func=COPY, scale=cos32[:, d : d + 1])
+            nc.vector.scalar_tensor_tensor(
+                out=dq[:, slot],
+                in0=g_il[:, :, partner, :],
+                scalar=sinr32[:, d : d + 1],
+                in1=g_cos[:, slot],
+                op0=MULT,
+                op1=ADD,
+            )
+            if slot >= Q_LAG and (slot - Q_LAG + 1) % GROUP == 0:
+                q = (slot - Q_LAG) // GROUP
+                quantise_and_multiply(q)
+                if q >= 1:
+                    empty_and_store(q - 1)
+        quantise_and_multiply(n_groups - 1)
+        empty_and_store(n_groups - 2)
+        empty_and_store(n_groups - 1)

@@ -1,6 +1,7 @@
 from contextlib import ExitStack
 
 import concourse.mybir as mybir
+from concourse.masks import make_identity
 
 BF16 = mybir.dt.bfloat16
 F32 = mybir.dt.float32
@@ -18,25 +19,34 @@ BATCH, SEQ, DIM, HEADS, HEAD_DIM = 4, 128, 128, 16, 128
 HALF = HEAD_DIM // 2
 PACK = 4
 N_MOVING = 512
-CHUNK_HEADS = 4
-N_CHUNKS = HEADS // CHUNK_HEADS
-WINDOW = 8
-N_WINDOWS = HEAD_DIM // WINDOW
-GROUP = 16
+CHUNK_HEADS = 2
+TILE_HEADS = 8
+FEAT_HEADS = HEADS - TILE_HEADS
+N_CHUNKS = TILE_HEADS // CHUNK_HEADS
+QUAD = 4
+N_QUADS = FEAT_HEADS // QUAD
+QUARTER = P // QUAD
+N_QUARTERS = HEAD_DIM // QUARTER
 Q_LAG = 2
-SPLIT = 84
-STORE_WINDOWS = 4
+EMPTY_AT = (40, 72)
 
 FLOPS = 2 * BATCH * SEQ * HEADS * HEAD_DIM * DIM
 BYTES = 2 * (BATCH * SEQ * DIM + 2 * SEQ * HEAD_DIM + BATCH * HEADS * SEQ * HEAD_DIM) + 4 * HEADS * HEAD_DIM * DIM
+
+
+def over_heads_and_batches(table):
+    n = table.shape[1]
+    return table.unsqueeze(1).unsqueeze(3).to_broadcast([P, CHUNK_HEADS, n, PACK])
 
 
 def tile_attention_pa_s_kernel(tc, query, wq, bq, cos, sin, grad_out, out):
     nc = tc.nc
     with ExitStack() as ctx:
         const = ctx.enter_context(tc.tile_pool(name="const", bufs=1))
-        loads = ctx.enter_context(tc.tile_pool(name="loads", bufs=N_CHUNKS))
-        acc_psum = ctx.enter_context(tc.psum_pool(name="acc_psum", bufs=6))
+        const_psum = ctx.enter_context(tc.psum_pool(name="const_psum", bufs=1))
+        loads = ctx.enter_context(tc.tile_pool(name="loads", bufs=2 * N_CHUNKS))
+        work = ctx.enter_context(tc.tile_pool(name="work", bufs=3))
+        acc_psum = ctx.enter_context(tc.psum_pool(name="acc_psum", bufs=7))
         ctx.enter_context(tc.manual_schedule())
 
         x_codes = const.tile([P, N_MOVING], U32, align_bytes=64)
@@ -46,101 +56,182 @@ def tile_attention_pa_s_kernel(tc, query, wq, bq, cos, sin, grad_out, out):
         nc.vector.memset(x_codes[:, DIM:N_MOVING].bitcast(I32), 0)
         nc.vector.memset(x_scales[:, DIM:N_MOVING].bitcast(I32), 0)
 
-        cos_raw = const.tile([P, HEAD_DIM], BF16)
+        tables = const.tile([P, 2, HEAD_DIM], BF16)
         sin_raw = const.tile([P, HEAD_DIM], BF16)
         x_raw = const.tile([P, BATCH, DIM], BF16)
-        nc.scalar.dma_start(out=cos_raw[:], in_=cos.rearrange("a b s d -> (a b s) d"))
+        nc.scalar.dma_start(out=tables[:, 0, :], in_=cos.rearrange("a b s d -> (a b s) d"))
         nc.scalar.dma_start(out=sin_raw[:], in_=sin.rearrange("a b s d -> (a b s) d"))
-        g_of_chunk = []
-        for c in range(N_CHUNKS):
+
+        def load(first_head):
             g = loads.tile([P, BATCH, CHUNK_HEADS, HEAD_DIM], BF16)
             for b in range(BATCH):
                 nc.sync.dma_start(
                     out=g[:, b],
-                    in_=grad_out[b, c * CHUNK_HEADS : (c + 1) * CHUNK_HEADS].rearrange("h s d -> s h d"),
+                    in_=grad_out[b, first_head : first_head + CHUNK_HEADS].rearrange("h s d -> s h d"),
                 )
-            g_of_chunk.append(g)
-            if c == 0:
+            return g
+
+        g_tile_road = []
+        g_feat_road = []
+        for c in range(N_CHUNKS):
+            g_tile_road.append(load(c * CHUNK_HEADS))
+            g_feat_road.append(load(TILE_HEADS + c * CHUNK_HEADS))
+            if c == 1:
                 nc.sync.dma_start(out=x_raw[:], in_=query.rearrange("b s i -> s b i"))
 
-        cos32 = const.tile([P, HEAD_DIM], F32)
-        sinr32 = const.tile([P, HEAD_DIM], F32)
-        nc.vector.tensor_copy(out=cos32[:], in_=cos_raw[:])
-        nc.vector.tensor_copy(out=sinr32[:, 0:HALF], in_=sin_raw[:, HALF:HEAD_DIM])
-        nc.vector.tensor_scalar_mul(out=sinr32[:, HALF:HEAD_DIM], in0=sin_raw[:, 0:HALF], scalar1=-1.0)
+        identity = const.tile([P, P], BF16)
+        make_identity(nc, identity[:])
+        nc.vector.tensor_copy(out=tables[:, 1, 0:HALF], in_=sin_raw[:, HALF:HEAD_DIM])
+        nc.vector.tensor_scalar_mul(out=tables[:, 1, HALF:HEAD_DIM], in0=sin_raw[:, 0:HALF], scalar1=-1.0)
+        tables_psum = const_psum.tile([P, 2, HEAD_DIM], F32)
+        nc.tensor.matmul(
+            out=tables_psum[:].rearrange("p t d -> p (t d)"),
+            lhsT=identity[:],
+            rhs=tables[:].rearrange("p t d -> p (t d)"),
+            start=True,
+            stop=True,
+        )
+        tables32 = const.tile([P, 2, HEAD_DIM], F32)
+        nc.vector.tensor_copy(out=tables32[:], in_=tables[:])
 
-        g_il = const.tile([P, HEADS, HEAD_DIM, PACK], BF16)
+        out_by_head = out.rearrange("(h d) i -> d h i", d=HEAD_DIM)
+        out_feat = out.rearrange(
+            "(e a l q m) i -> e l q m a i", e=HEADS // FEAT_HEADS, a=N_QUADS, l=QUAD, q=N_QUARTERS, m=QUARTER
+        )
+        products_of_chunk = []
+        dq_tile = const.tile([P, TILE_HEADS, HEAD_DIM, PACK], BF16, align_bytes=64)
+        result_tile = const.tile([P, TILE_HEADS, DIM], F32)
+        g_il = const.tile([P, FEAT_HEADS, HEAD_DIM, PACK], BF16)
         x_grouped = const.tile([P, DIM, PACK], BF16, align_bytes=64)
-        for c in range(N_CHUNKS):
-            heads = slice(c * CHUNK_HEADS, (c + 1) * CHUNK_HEADS)
-            g_words = g_of_chunk[c][:].rearrange("p b h d -> p h d b")
-            nc.vector.tensor_copy(out=g_il[:, heads, 0:SPLIT, :], in_=g_words[:, :, 0:SPLIT, :])
-            nc.scalar.copy(out=g_il[:, heads, SPLIT:HEAD_DIM, :], in_=g_words[:, :, SPLIT:HEAD_DIM, :])
-            if c == 0:
-                nc.scalar.copy(out=x_grouped[:], in_=x_raw[:].rearrange("p b i -> p i b"))
-            if c == 1:
-                nc.vector.quantize_mx(
-                    out=x_codes[:, 0:DIM].bitcast(E4M3_X4),
-                    scales=x_scales[:, 0:DIM],
-                    in_=x_grouped[:].rearrange("p i b -> p (i b)"),
-                )
+        g_cos_feat = const.tile([P, HEAD_DIM, FEAT_HEADS, PACK], F32)
+        dq_feat = const.tile([P, N_QUARTERS, N_QUADS, QUARTER, QUAD, PACK], BF16, align_bytes=64)
+        result_feat = const.tile([P, N_QUARTERS, N_QUADS, DIM], F32)
 
-        g_cos = const.tile([P, HEAD_DIM, HEADS, PACK], F32)
-        dq = const.tile([P, HEAD_DIM, HEADS, PACK], BF16, align_bytes=64)
-        result = const.tile([P, N_WINDOWS, DIM], F32)
-        out_view = out.rearrange("(h dl j) i -> dl h j i", h=HEADS, dl=WINDOW, j=N_WINDOWS)
-        acc_of_window = {}
+        def products(c):
+            table_source = tables if c == 0 else tables_psum
+            g_words = g_tile_road[c][:].rearrange("p b h d -> p h d b")
+            g_cos = work.tile([P, CHUNK_HEADS, HEAD_DIM, PACK], F32)
+            g_sin = work.tile([P, CHUNK_HEADS, HEAD_DIM, PACK], F32)
+            nc.vector.tensor_tensor(
+                out=g_cos[:], in0=g_words, in1=over_heads_and_batches(table_source[:, 0, :]), op=MULT
+            )
+            nc.vector.tensor_tensor(
+                out=g_sin[:, :, 0:HALF, :],
+                in0=g_words[:, :, HALF:HEAD_DIM, :],
+                in1=over_heads_and_batches(table_source[:, 1, 0:HALF]),
+                op=MULT,
+            )
+            nc.vector.tensor_tensor(
+                out=g_sin[:, :, HALF:HEAD_DIM, :],
+                in0=g_words[:, :, 0:HALF, :],
+                in1=over_heads_and_batches(table_source[:, 1, HALF:HEAD_DIM]),
+                op=MULT,
+            )
+            products_of_chunk.append((g_cos, g_sin))
 
-        def quantise_and_multiply(q):
-            slots = slice(q * GROUP, (q + 1) * GROUP)
-            columns = slice(q * GROUP * HEADS, (q + 1) * GROUP * HEADS)
+        def add(c):
+            g_cos, g_sin = products_of_chunk[c]
+            engine = nc.vector if c == N_CHUNKS - 1 else nc.gpsimd
+            engine.tensor_tensor(
+                out=dq_tile[:, c * CHUNK_HEADS : (c + 1) * CHUNK_HEADS], in0=g_cos[:], in1=g_sin[:], op=ADD
+            )
+
+        def interleave(c):
+            nc.scalar.copy(
+                out=g_il[:, c * CHUNK_HEADS : (c + 1) * CHUNK_HEADS],
+                in_=g_feat_road[c][:].rearrange("p b h d -> p h d b"),
+            )
+
+        def multiply(first_column):
+            columns = slice(first_column, first_column + P)
+            acc = acc_psum.tile([P, N_MOVING], F32)
+            nc.tensor.matmul_mx(
+                out=acc[:],
+                lhsT=dp_codes[:, columns].bitcast(E5M2_X4),
+                lhsT_scale=dp_scales[:, columns],
+                rhs=x_codes[:].bitcast(E4M3_X4),
+                rhs_scale=x_scales[:],
+                start=True,
+                stop=True,
+            )
+            return acc
+
+        acc_of_head = {}
+
+        def quantise_tile_road(first_head, n_heads):
+            columns = slice(first_head * HEAD_DIM, (first_head + n_heads) * HEAD_DIM)
             nc.vector.quantize_mx(
                 out=dp_codes[:, columns].bitcast(E5M2_X4),
                 scales=dp_scales[:, columns],
-                in_=dq[:, slots].rearrange("p s h b -> p (s h b)"),
+                in_=dq_tile[:, first_head : first_head + n_heads].rearrange("p h d b -> p (h d b)"),
             )
-            for j in range(q * GROUP // WINDOW, (q + 1) * GROUP // WINDOW):
-                window_columns = slice(j * P, (j + 1) * P)
-                acc = acc_psum.tile([P, N_MOVING], F32)
-                nc.tensor.matmul_mx(
-                    out=acc[:],
-                    lhsT=dp_codes[:, window_columns].bitcast(E5M2_X4),
-                    lhsT_scale=dp_scales[:, window_columns],
-                    rhs=x_codes[:].bitcast(E4M3_X4),
-                    rhs_scale=x_scales[:],
-                    start=True,
-                    stop=True,
-                )
-                acc_of_window[j] = acc
+            for h in range(first_head, first_head + n_heads):
+                acc_of_head[h] = multiply(h * HEAD_DIM)
 
-        def empty_and_store(q):
-            for j in range(q * GROUP // WINDOW, (q + 1) * GROUP // WINDOW):
-                nc.scalar.copy(out=result[:, j, :], in_=acc_of_window[j][:, 0:DIM])
-                if (j + 1) % STORE_WINDOWS == 0:
-                    windows = slice(j + 1 - STORE_WINDOWS, j + 1)
-                    for dl in range(WINDOW):
-                        rows = slice(dl * HEADS, (dl + 1) * HEADS)
-                        nc.sync.dma_start(out=out_view[dl, :, windows, :], in_=result[rows, windows, :])
+        def empty_tile_road(first_head, n_heads):
+            for h in range(first_head, first_head + n_heads):
+                nc.scalar.copy(out=result_tile[:, h, :], in_=acc_of_head[h][:, 0:DIM])
+            heads = slice(first_head, first_head + n_heads)
+            nc.sync.dma_start(out=out_by_head[:, heads, :], in_=result_tile[:, heads, :])
 
-        n_groups = HEAD_DIM // GROUP
-        for slot in range(HEAD_DIM):
-            j, dl = slot // WINDOW, slot % WINDOW
-            d = N_WINDOWS * dl + j
+        products(0)
+        interleave(0)
+        for c in range(N_CHUNKS - 1):
+            add(c)
+            products(c + 1)
+            if c == 1:
+                nc.scalar.copy(out=x_grouped[:], in_=x_raw[:].rearrange("p b i -> p i b"))
+            interleave(c + 1)
+        nc.vector.quantize_mx(
+            out=x_codes[:, 0:DIM].bitcast(E4M3_X4),
+            scales=x_scales[:, 0:DIM],
+            in_=x_grouped[:].rearrange("p i b -> p (i b)"),
+        )
+        quantise_tile_road(0, TILE_HEADS // 2)
+        add(N_CHUNKS - 1)
+        quantise_tile_road(TILE_HEADS // 2, TILE_HEADS // 2)
+
+        for d in range(HEAD_DIM):
+            nc.scalar.activation(
+                out=g_cos_feat[:, d], in_=g_il[:, :, d, :], func=COPY, scale=tables32[:, 0, d : d + 1]
+            )
+            if d == EMPTY_AT[0]:
+                empty_tile_road(0, TILE_HEADS // 2)
+            if d == EMPTY_AT[1]:
+                empty_tile_road(TILE_HEADS // 2, TILE_HEADS // 2)
+
+        acc_of_window = {}
+
+        def quantise_feat_road(q):
+            first_column = TILE_HEADS * HEAD_DIM + q * N_QUADS * P
+            columns = slice(first_column, first_column + N_QUADS * P)
+            nc.vector.quantize_mx(
+                out=dp_codes[:, columns].bitcast(E5M2_X4),
+                scales=dp_scales[:, columns],
+                in_=dq_feat[:, q].rearrange("p a m l b -> p (a m l b)"),
+            )
+            for a in range(N_QUADS):
+                acc_of_window[(q, a)] = multiply(first_column + a * P)
+
+        def empty_feat_road(q):
+            for a in range(N_QUADS):
+                nc.scalar.copy(out=result_feat[:, q, a, :], in_=acc_of_window[(q, a)][:, 0:DIM])
+            for l in range(QUAD):
+                nc.sync.dma_start(out=out_feat[1, l, q], in_=result_feat[l:P:QUAD, q, :, :])
+
+        for d in range(HEAD_DIM):
             partner = d + HALF if d < HALF else d - HALF
-            nc.scalar.activation(out=g_cos[:, slot], in_=g_il[:, :, d, :], func=COPY, scale=cos32[:, d : d + 1])
             nc.vector.scalar_tensor_tensor(
-                out=dq[:, slot],
-                in0=g_il[:, :, partner, :],
-                scalar=sinr32[:, d : d + 1],
-                in1=g_cos[:, slot],
+                out=dq_feat[:, d // QUARTER, :, d % QUARTER, :, :],
+                in0=g_il[:, :, partner, :].rearrange("p (a l) b -> p a l b", a=N_QUADS),
+                scalar=tables32[:, 1, d : d + 1],
+                in1=g_cos_feat[:, d].rearrange("p (a l) b -> p a l b", a=N_QUADS),
                 op0=MULT,
                 op1=ADD,
             )
-            if slot >= Q_LAG and (slot - Q_LAG + 1) % GROUP == 0:
-                q = (slot - Q_LAG) // GROUP
-                quantise_and_multiply(q)
-                if q >= 1:
-                    empty_and_store(q - 1)
-        quantise_and_multiply(n_groups - 1)
-        empty_and_store(n_groups - 2)
-        empty_and_store(n_groups - 1)
+            if d >= Q_LAG and (d - Q_LAG + 1) % QUARTER == 0:
+                q = (d - Q_LAG) // QUARTER
+                quantise_feat_road(q)
+                empty_feat_road(q)
+        quantise_feat_road(N_QUARTERS - 1)
+        empty_feat_road(N_QUARTERS - 1)

@@ -29,6 +29,7 @@ QUARTER = P // QUAD
 N_QUARTERS = HEAD_DIM // QUARTER
 Q_LAG = 2
 EMPTY_AT = (40, 72)
+LOAD_ORDER = ("tile", "tile", "feat", "tile", "feat", "x", "tile", "feat", "feat")
 
 FLOPS = 2 * BATCH * SEQ * HEADS * HEAD_DIM * DIM
 BYTES = 2 * (BATCH * SEQ * DIM + 2 * SEQ * HEAD_DIM + BATCH * HEADS * SEQ * HEAD_DIM) + 4 * HEADS * HEAD_DIM * DIM
@@ -73,10 +74,12 @@ def tile_attention_pa_s_kernel(tc, query, wq, bq, cos, sin, grad_out, out):
 
         g_tile_road = []
         g_feat_road = []
-        for c in range(N_CHUNKS):
-            g_tile_road.append(load(c * CHUNK_HEADS))
-            g_feat_road.append(load(TILE_HEADS + c * CHUNK_HEADS))
-            if c == 1:
+        for road in LOAD_ORDER:
+            if road == "tile":
+                g_tile_road.append(load(len(g_tile_road) * CHUNK_HEADS))
+            elif road == "feat":
+                g_feat_road.append(load(TILE_HEADS + len(g_feat_road) * CHUNK_HEADS))
+            else:
                 nc.sync.dma_start(out=x_raw[:], in_=query.rearrange("b s i -> s b i"))
 
         identity = const.tile([P, P], BF16)

@@ -29,7 +29,7 @@ QUARTER = P // QUAD
 N_QUARTERS = HEAD_DIM // QUARTER
 Q_LAG = 2
 EMPTY_AT = (40, 72)
-LOAD_ORDER = ("tile", "tile", "feat", "tile", "feat", "x", "tile", "feat", "feat")
+LOAD_ORDER = ((0, 2), (2, 2), (4, 4), (8, 4), (0, 0), (12, 4))
 
 FLOPS = 2 * BATCH * SEQ * HEADS * HEAD_DIM * DIM
 BYTES = 2 * (BATCH * SEQ * DIM + 2 * SEQ * HEAD_DIM + BATCH * HEADS * SEQ * HEAD_DIM) + 4 * HEADS * HEAD_DIM * DIM
@@ -45,7 +45,6 @@ def tile_attention_pa_s_kernel(tc, query, wq, bq, cos, sin, grad_out, out):
     with ExitStack() as ctx:
         const = ctx.enter_context(tc.tile_pool(name="const", bufs=1))
         const_psum = ctx.enter_context(tc.psum_pool(name="const_psum", bufs=1))
-        loads = ctx.enter_context(tc.tile_pool(name="loads", bufs=2 * N_CHUNKS))
         work = ctx.enter_context(tc.tile_pool(name="work", bufs=3))
         acc_psum = ctx.enter_context(tc.psum_pool(name="acc_psum", bufs=7))
         ctx.enter_context(tc.manual_schedule())
@@ -63,24 +62,18 @@ def tile_attention_pa_s_kernel(tc, query, wq, bq, cos, sin, grad_out, out):
         nc.scalar.dma_start(out=tables[:, 0, :], in_=cos.rearrange("a b s d -> (a b s) d"))
         nc.scalar.dma_start(out=sin_raw[:], in_=sin.rearrange("a b s d -> (a b s) d"))
 
-        def load(first_head):
-            g = loads.tile([P, BATCH, CHUNK_HEADS, HEAD_DIM], BF16)
-            for b in range(BATCH):
-                nc.sync.dma_start(
-                    out=g[:, b],
-                    in_=grad_out[b, first_head : first_head + CHUNK_HEADS].rearrange("h s d -> s h d"),
-                )
-            return g
+        g_all = const.tile([P, BATCH, HEADS, HEAD_DIM], BF16)
 
-        g_tile_road = []
-        g_feat_road = []
-        for road in LOAD_ORDER:
-            if road == "tile":
-                g_tile_road.append(load(len(g_tile_road) * CHUNK_HEADS))
-            elif road == "feat":
-                g_feat_road.append(load(TILE_HEADS + len(g_feat_road) * CHUNK_HEADS))
-            else:
+        def load(first_head, n_heads):
+            heads = slice(first_head, first_head + n_heads)
+            for b in range(BATCH):
+                nc.sync.dma_start(out=g_all[:, b, heads, :], in_=grad_out[b, heads].rearrange("h s d -> s h d"))
+
+        for first_head, n_heads in LOAD_ORDER:
+            if n_heads == 0:
                 nc.sync.dma_start(out=x_raw[:], in_=query.rearrange("b s i -> s b i"))
+            else:
+                load(first_head, n_heads)
 
         identity = const.tile([P, P], BF16)
         make_identity(nc, identity[:])
@@ -112,7 +105,7 @@ def tile_attention_pa_s_kernel(tc, query, wq, bq, cos, sin, grad_out, out):
 
         def products(c):
             table_source = tables if c == 0 else tables_psum
-            g_words = g_tile_road[c][:].rearrange("p b h d -> p h d b")
+            g_words = g_all[:, :, c * CHUNK_HEADS : (c + 1) * CHUNK_HEADS, :].rearrange("p b h d -> p h d b")
             g_cos = work.tile([P, CHUNK_HEADS, HEAD_DIM, PACK], F32)
             g_sin = work.tile([P, CHUNK_HEADS, HEAD_DIM, PACK], F32)
             nc.vector.tensor_tensor(
@@ -142,7 +135,9 @@ def tile_attention_pa_s_kernel(tc, query, wq, bq, cos, sin, grad_out, out):
         def interleave(c):
             nc.scalar.copy(
                 out=g_il[:, c * CHUNK_HEADS : (c + 1) * CHUNK_HEADS],
-                in_=g_feat_road[c][:].rearrange("p b h d -> p h d b"),
+                in_=g_all[
+                    :, :, TILE_HEADS + c * CHUNK_HEADS : TILE_HEADS + (c + 1) * CHUNK_HEADS, :
+                ].rearrange("p b h d -> p h d b"),
             )
 
         def multiply(first_column):

@@ -19,25 +19,25 @@ BATCH, SEQ, DIM, HEADS, HEAD_DIM = 4, 128, 128, 16, 128
 HALF = HEAD_DIM // 2
 PACK = 4
 N_MOVING = 512
-CHUNK_HEADS = 2
-TILE_HEADS = 8
-FEAT_HEADS = HEADS - TILE_HEADS
-N_CHUNKS = TILE_HEADS // CHUNK_HEADS
+BAND = 32
+ROAD = 2 * BAND
 QUAD = 4
-N_QUADS = FEAT_HEADS // QUAD
-QUARTER = P // QUAD
-N_QUARTERS = HEAD_DIM // QUARTER
+N_QUADS = HEADS // QUAD
+PAIR = 2
+N_PAIRS = HEADS // PAIR
+MAX_CHUNK = 4
+CHUNKS = ((0, 2), (2, 2), (4, 4), (8, 4), (12, 2), (14, 2))
+X_BEHIND = 2
 Q_LAG = 2
-EMPTY_AT = (40, 72)
-LOAD_ORDER = ((0, 2), (2, 2), (4, 4), (8, 4), (0, 0), (12, 4))
+EMPTY_AT = {31: (0, 6), 47: (6, 2)}
 
 FLOPS = 2 * BATCH * SEQ * HEADS * HEAD_DIM * DIM
 BYTES = 2 * (BATCH * SEQ * DIM + 2 * SEQ * HEAD_DIM + BATCH * HEADS * SEQ * HEAD_DIM) + 4 * HEADS * HEAD_DIM * DIM
 
 
-def over_heads_and_batches(table):
+def over_heads_and_batches(table, n_heads):
     n = table.shape[1]
-    return table.unsqueeze(1).unsqueeze(3).to_broadcast([P, CHUNK_HEADS, n, PACK])
+    return table.unsqueeze(1).unsqueeze(3).to_broadcast([P, n_heads, n, PACK])
 
 
 def tile_attention_pa_s_kernel(tc, query, wq, bq, cos, sin, grad_out, out):
@@ -63,17 +63,12 @@ def tile_attention_pa_s_kernel(tc, query, wq, bq, cos, sin, grad_out, out):
         nc.scalar.dma_start(out=sin_raw[:], in_=sin.rearrange("a b s d -> (a b s) d"))
 
         g_all = const.tile([P, BATCH, HEADS, HEAD_DIM], BF16)
-
-        def load(first_head, n_heads):
+        for c, (first_head, n_heads) in enumerate(CHUNKS):
             heads = slice(first_head, first_head + n_heads)
             for b in range(BATCH):
                 nc.sync.dma_start(out=g_all[:, b, heads, :], in_=grad_out[b, heads].rearrange("h s d -> s h d"))
-
-        for first_head, n_heads in LOAD_ORDER:
-            if n_heads == 0:
+            if c == X_BEHIND:
                 nc.sync.dma_start(out=x_raw[:], in_=query.rearrange("b s i -> s b i"))
-            else:
-                load(first_head, n_heads)
 
         identity = const.tile([P, P], BF16)
         make_identity(nc, identity[:])
@@ -90,55 +85,64 @@ def tile_attention_pa_s_kernel(tc, query, wq, bq, cos, sin, grad_out, out):
         tables32 = const.tile([P, 2, HEAD_DIM], F32)
         nc.vector.tensor_copy(out=tables32[:], in_=tables[:])
 
-        out_by_head = out.rearrange("(h d) i -> d h i", d=HEAD_DIM)
-        out_feat = out.rearrange(
-            "(e a l q m) i -> e l q m a i", e=HEADS // FEAT_HEADS, a=N_QUADS, l=QUAD, q=N_QUARTERS, m=QUARTER
-        )
+        out_feat = out.rearrange("(a l u z m) i -> l u z m a i", a=N_QUADS, l=QUAD, u=2, z=2, m=BAND)
+        out_tile = out.rearrange("(w v u z k) i -> v u z k w i", w=N_PAIRS, v=PAIR, u=2, z=2, k=BAND)
         products_of_chunk = []
-        dq_tile = const.tile([P, TILE_HEADS, HEAD_DIM, PACK], BF16, align_bytes=64)
-        result_tile = const.tile([P, TILE_HEADS, DIM], F32)
-        g_il = const.tile([P, FEAT_HEADS, HEAD_DIM, PACK], BF16)
+        dq_tile = const.tile([P, HEADS, ROAD, PACK], BF16, align_bytes=64)
+        result_tile = const.tile([P, N_PAIRS, DIM], F32)
+        g_il = const.tile([P, HEADS, ROAD, PACK], BF16)
         x_grouped = const.tile([P, DIM, PACK], BF16, align_bytes=64)
-        g_cos_feat = const.tile([P, HEAD_DIM, FEAT_HEADS, PACK], F32)
-        dq_feat = const.tile([P, N_QUARTERS, N_QUADS, QUARTER, QUAD, PACK], BF16, align_bytes=64)
-        result_feat = const.tile([P, N_QUARTERS, N_QUADS, DIM], F32)
+        g_cos_feat = const.tile([P, ROAD, HEADS, PACK], F32)
+        dq_feat = const.tile([P, 2, N_QUADS, BAND, QUAD, PACK], BF16, align_bytes=64)
+        result_feat = const.tile([P, 2, N_QUADS, DIM], F32)
+
+        def words(c):
+            first_head, n_heads = CHUNKS[c]
+            return g_all[:, :, first_head : first_head + n_heads, :].rearrange("p b h d -> p h d b")
 
         def products(c):
+            n_heads = CHUNKS[c][1]
             table_source = tables if c == 0 else tables_psum
-            g_words = g_all[:, :, c * CHUNK_HEADS : (c + 1) * CHUNK_HEADS, :].rearrange("p b h d -> p h d b")
-            g_cos = work.tile([P, CHUNK_HEADS, HEAD_DIM, PACK], F32)
-            g_sin = work.tile([P, CHUNK_HEADS, HEAD_DIM, PACK], F32)
-            nc.vector.tensor_tensor(
-                out=g_cos[:], in0=g_words, in1=over_heads_and_batches(table_source[:, 0, :]), op=MULT
-            )
-            nc.vector.tensor_tensor(
-                out=g_sin[:, :, 0:HALF, :],
-                in0=g_words[:, :, HALF:HEAD_DIM, :],
-                in1=over_heads_and_batches(table_source[:, 1, 0:HALF]),
-                op=MULT,
-            )
-            nc.vector.tensor_tensor(
-                out=g_sin[:, :, HALF:HEAD_DIM, :],
-                in0=g_words[:, :, 0:HALF, :],
-                in1=over_heads_and_batches(table_source[:, 1, HALF:HEAD_DIM]),
-                op=MULT,
-            )
+            g_words = words(c)
+            g_cos = work.tile([P, MAX_CHUNK, ROAD, PACK], F32)
+            g_sin = work.tile([P, MAX_CHUNK, ROAD, PACK], F32)
+            for u in range(2):
+                band = slice(HALF * u + BAND, HALF * u + 2 * BAND)
+                partner = slice(HALF * (1 - u) + BAND, HALF * (1 - u) + 2 * BAND)
+                place = slice(BAND * u, BAND * (u + 1))
+                nc.vector.tensor_tensor(
+                    out=g_cos[:, 0:n_heads, place, :],
+                    in0=g_words[:, :, band, :],
+                    in1=over_heads_and_batches(table_source[:, 0, band], n_heads),
+                    op=MULT,
+                )
+                nc.vector.tensor_tensor(
+                    out=g_sin[:, 0:n_heads, place, :],
+                    in0=g_words[:, :, partner, :],
+                    in1=over_heads_and_batches(table_source[:, 1, band], n_heads),
+                    op=MULT,
+                )
             products_of_chunk.append((g_cos, g_sin))
 
         def add(c):
+            first_head, n_heads = CHUNKS[c]
             g_cos, g_sin = products_of_chunk[c]
-            engine = nc.vector if c == N_CHUNKS - 1 else nc.gpsimd
+            engine = nc.vector if c == len(CHUNKS) - 1 else nc.gpsimd
             engine.tensor_tensor(
-                out=dq_tile[:, c * CHUNK_HEADS : (c + 1) * CHUNK_HEADS], in0=g_cos[:], in1=g_sin[:], op=ADD
+                out=dq_tile[:, first_head : first_head + n_heads],
+                in0=g_cos[:, 0:n_heads],
+                in1=g_sin[:, 0:n_heads],
+                op=ADD,
             )
 
         def interleave(c):
-            nc.scalar.copy(
-                out=g_il[:, c * CHUNK_HEADS : (c + 1) * CHUNK_HEADS],
-                in_=g_all[
-                    :, :, TILE_HEADS + c * CHUNK_HEADS : TILE_HEADS + (c + 1) * CHUNK_HEADS, :
-                ].rearrange("p b h d -> p h d b"),
-            )
+            first_head, n_heads = CHUNKS[c]
+            g_words = words(c)
+            for u in range(2):
+                nc.scalar.copy(
+                    out=g_il[:, first_head : first_head + n_heads, BAND * u : BAND * (u + 1), :],
+                    in_=g_words[:, :, HALF * u : HALF * u + BAND, :],
+                )
 
         def multiply(first_column):
             columns = slice(first_column, first_column + P)
@@ -154,30 +158,34 @@ def tile_attention_pa_s_kernel(tc, query, wq, bq, cos, sin, grad_out, out):
             )
             return acc
 
-        acc_of_head = {}
+        acc_of_pair = {}
 
-        def quantise_tile_road(first_head, n_heads):
-            columns = slice(first_head * HEAD_DIM, (first_head + n_heads) * HEAD_DIM)
+        def quantise_tile_road(first_pair, n_pairs):
+            columns = slice(first_pair * P, (first_pair + n_pairs) * P)
             nc.vector.quantize_mx(
                 out=dp_codes[:, columns].bitcast(E5M2_X4),
                 scales=dp_scales[:, columns],
-                in_=dq_tile[:, first_head : first_head + n_heads].rearrange("p h d b -> p (h d b)"),
+                in_=dq_tile[:, first_pair * PAIR : (first_pair + n_pairs) * PAIR].rearrange("p h e b -> p (h e b)"),
             )
-            for h in range(first_head, first_head + n_heads):
-                acc_of_head[h] = multiply(h * HEAD_DIM)
+            for w in range(first_pair, first_pair + n_pairs):
+                acc_of_pair[w] = multiply(w * P)
 
-        def empty_tile_road(first_head, n_heads):
-            for h in range(first_head, first_head + n_heads):
-                nc.scalar.copy(out=result_tile[:, h, :], in_=acc_of_head[h][:, 0:DIM])
-            heads = slice(first_head, first_head + n_heads)
-            nc.sync.dma_start(out=out_by_head[:, heads, :], in_=result_tile[:, heads, :])
+        def empty_tile_road(first_pair, n_pairs):
+            for w in range(first_pair, first_pair + n_pairs):
+                nc.scalar.copy(out=result_tile[:, w, :], in_=acc_of_pair[w][:, 0:DIM])
+            pairs = slice(first_pair, first_pair + n_pairs)
+            for v in range(PAIR):
+                for u in range(2):
+                    rows = slice(ROAD * v + BAND * u, ROAD * v + BAND * (u + 1))
+                    nc.sync.dma_start(out=out_tile[v, u, 1][:, pairs, :], in_=result_tile[rows, pairs, :])
 
+        last = len(CHUNKS) - 1
         products(0)
         interleave(0)
-        for c in range(N_CHUNKS - 1):
+        for c in range(last):
             add(c)
             products(c + 1)
-            if c == 1:
+            if c == X_BEHIND:
                 nc.scalar.copy(out=x_grouped[:], in_=x_raw[:].rearrange("p b i -> p i b"))
             interleave(c + 1)
         nc.vector.quantize_mx(
@@ -185,51 +193,49 @@ def tile_attention_pa_s_kernel(tc, query, wq, bq, cos, sin, grad_out, out):
             scales=x_scales[:, 0:DIM],
             in_=x_grouped[:].rearrange("p i b -> p (i b)"),
         )
-        quantise_tile_road(0, TILE_HEADS // 2)
-        add(N_CHUNKS - 1)
-        quantise_tile_road(TILE_HEADS // 2, TILE_HEADS // 2)
+        quantise_tile_road(0, N_PAIRS // 2)
+        add(last)
+        quantise_tile_road(N_PAIRS // 2, N_PAIRS // 2)
 
-        for d in range(HEAD_DIM):
+        for f in range(ROAD):
+            d = HALF * (f // BAND) + f % BAND
             nc.scalar.activation(
-                out=g_cos_feat[:, d], in_=g_il[:, :, d, :], func=COPY, scale=tables32[:, 0, d : d + 1]
+                out=g_cos_feat[:, f], in_=g_il[:, :, f, :], func=COPY, scale=tables32[:, 0, d : d + 1]
             )
-            if d == EMPTY_AT[0]:
-                empty_tile_road(0, TILE_HEADS // 2)
-            if d == EMPTY_AT[1]:
-                empty_tile_road(TILE_HEADS // 2, TILE_HEADS // 2)
+            if f in EMPTY_AT:
+                empty_tile_road(EMPTY_AT[f][0], EMPTY_AT[f][1])
 
         acc_of_window = {}
 
-        def quantise_feat_road(q):
-            first_column = TILE_HEADS * HEAD_DIM + q * N_QUADS * P
-            columns = slice(first_column, first_column + N_QUADS * P)
-            nc.vector.quantize_mx(
-                out=dp_codes[:, columns].bitcast(E5M2_X4),
-                scales=dp_scales[:, columns],
-                in_=dq_feat[:, q].rearrange("p a m l b -> p (a m l b)"),
-            )
+        def quantise_feat_road(u):
             for a in range(N_QUADS):
-                acc_of_window[(q, a)] = multiply(first_column + a * P)
+                first_column = HEADS * ROAD + (u * N_QUADS + a) * P
+                columns = slice(first_column, first_column + P)
+                nc.vector.quantize_mx(
+                    out=dp_codes[:, columns].bitcast(E5M2_X4),
+                    scales=dp_scales[:, columns],
+                    in_=dq_feat[:, u, a].rearrange("p m l b -> p (m l b)"),
+                )
+                acc_of_window[(u, a)] = multiply(first_column)
 
-        def empty_feat_road(q):
+        def empty_feat_road(u):
             for a in range(N_QUADS):
-                nc.scalar.copy(out=result_feat[:, q, a, :], in_=acc_of_window[(q, a)][:, 0:DIM])
+                nc.scalar.copy(out=result_feat[:, u, a, :], in_=acc_of_window[(u, a)][:, 0:DIM])
             for l in range(QUAD):
-                nc.sync.dma_start(out=out_feat[1, l, q], in_=result_feat[l:P:QUAD, q, :, :])
+                nc.sync.dma_start(out=out_feat[l, u, 0], in_=result_feat[l:P:QUAD, u, :, :])
 
-        for d in range(HEAD_DIM):
-            partner = d + HALF if d < HALF else d - HALF
+        for f in range(ROAD):
+            d = HALF * (f // BAND) + f % BAND
             nc.vector.scalar_tensor_tensor(
-                out=dq_feat[:, d // QUARTER, :, d % QUARTER, :, :],
-                in0=g_il[:, :, partner, :].rearrange("p (a l) b -> p a l b", a=N_QUADS),
+                out=dq_feat[:, f // BAND, :, f % BAND, :, :],
+                in0=g_il[:, :, (f + BAND) % ROAD, :].rearrange("p (a l) b -> p a l b", a=N_QUADS),
                 scalar=tables32[:, 1, d : d + 1],
-                in1=g_cos_feat[:, d].rearrange("p (a l) b -> p a l b", a=N_QUADS),
+                in1=g_cos_feat[:, f].rearrange("p (a l) b -> p a l b", a=N_QUADS),
                 op0=MULT,
                 op1=ADD,
             )
-            if d >= Q_LAG and (d - Q_LAG + 1) % QUARTER == 0:
-                q = (d - Q_LAG) // QUARTER
-                quantise_feat_road(q)
-                empty_feat_road(q)
-        quantise_feat_road(N_QUARTERS - 1)
-        empty_feat_road(N_QUARTERS - 1)
+            if f == BAND - 1 + Q_LAG:
+                quantise_feat_road(0)
+                empty_feat_road(0)
+        quantise_feat_road(1)
+        empty_feat_road(1)

from contextlib import ExitStack

import concourse.mybir as mybir
from concourse.masks import make_identity

BF16 = mybir.dt.bfloat16
F32 = mybir.dt.float32
I32 = mybir.dt.int32
U32 = mybir.dt.uint32
U8 = mybir.dt.uint8
E4M3_X4 = mybir.dt.float8_e4m3fn_x4
E5M2_X4 = mybir.dt.float8_e5m2_x4
MULT = mybir.AluOpType.mult
ADD = mybir.AluOpType.add
COPY = mybir.ActivationFunctionType.Copy

P = 128
BATCH, SEQ, DIM, HEADS, HEAD_DIM = 4, 128, 128, 16, 128
HALF = HEAD_DIM // 2
PACK = 4
N_MOVING = 512
BAND = 32
ROAD = 2 * BAND
QUAD = 4
N_QUADS = HEADS // QUAD
PAIR = 2
N_PAIRS = HEADS // PAIR
MAX_CHUNK = 4
CHUNKS = ((0, 2), (2, 2), (4, 4), (8, 4), (12, 2), (14, 2))
X_BEHIND = 2
Q_LAG = 2
EMPTY_AT = {31: (0, 6), 47: (6, 2)}

FLOPS = 2 * BATCH * SEQ * HEADS * HEAD_DIM * DIM
BYTES = 2 * (BATCH * SEQ * DIM + 2 * SEQ * HEAD_DIM + BATCH * HEADS * SEQ * HEAD_DIM) + 4 * HEADS * HEAD_DIM * DIM


def over_heads_and_batches(table, n_heads):
    n = table.shape[1]
    return table.unsqueeze(1).unsqueeze(3).to_broadcast([P, n_heads, n, PACK])


def tile_attention_pa_s_kernel(tc, query, wq, bq, cos, sin, grad_out, out):
    nc = tc.nc
    with ExitStack() as ctx:
        const = ctx.enter_context(tc.tile_pool(name="const", bufs=1))
        const_psum = ctx.enter_context(tc.psum_pool(name="const_psum", bufs=1))
        work = ctx.enter_context(tc.tile_pool(name="work", bufs=3))
        acc_psum = ctx.enter_context(tc.psum_pool(name="acc_psum", bufs=7))
        ctx.enter_context(tc.manual_schedule())

        x_codes = const.tile([P, N_MOVING], U32, align_bytes=64)
        x_scales = const.tile([P, N_MOVING], U8, align_bytes=64)
        dp_codes = const.tile([P, HEADS * HEAD_DIM], U32, align_bytes=64)
        dp_scales = const.tile([P, HEADS * HEAD_DIM], U8, align_bytes=64)
        nc.vector.memset(x_codes[:, DIM:N_MOVING].bitcast(I32), 0)
        nc.vector.memset(x_scales[:, DIM:N_MOVING].bitcast(I32), 0)

        tables = const.tile([P, 2, HEAD_DIM], BF16)
        sin_raw = const.tile([P, HEAD_DIM], BF16)
        x_raw = const.tile([P, BATCH, DIM], BF16)
        nc.scalar.dma_start(out=tables[:, 0, :], in_=cos.rearrange("a b s d -> (a b s) d"))
        nc.scalar.dma_start(out=sin_raw[:], in_=sin.rearrange("a b s d -> (a b s) d"))

        g_all = const.tile([P, BATCH, HEADS, HEAD_DIM], BF16)
        for c, (first_head, n_heads) in enumerate(CHUNKS):
            heads = slice(first_head, first_head + n_heads)
            for b in range(BATCH):
                nc.sync.dma_start(out=g_all[:, b, heads, :], in_=grad_out[b, heads].rearrange("h s d -> s h d"))
            if c == X_BEHIND:
                nc.sync.dma_start(out=x_raw[:], in_=query.rearrange("b s i -> s b i"))

        identity = const.tile([P, P], BF16)
        make_identity(nc, identity[:])
        nc.vector.tensor_copy(out=tables[:, 1, 0:HALF], in_=sin_raw[:, HALF:HEAD_DIM])
        nc.vector.tensor_scalar_mul(out=tables[:, 1, HALF:HEAD_DIM], in0=sin_raw[:, 0:HALF], scalar1=-1.0)
        tables_psum = const_psum.tile([P, 2, HEAD_DIM], F32)
        nc.tensor.matmul(
            out=tables_psum[:].rearrange("p t d -> p (t d)"),
            lhsT=identity[:],
            rhs=tables[:].rearrange("p t d -> p (t d)"),
            start=True,
            stop=True,
        )
        tables32 = const.tile([P, 2, HEAD_DIM], F32)
        nc.vector.tensor_copy(out=tables32[:], in_=tables[:])

        out_feat = out.rearrange("(a l u z m) i -> l u z m a i", a=N_QUADS, l=QUAD, u=2, z=2, m=BAND)
        out_tile = out.rearrange("(w v u z k) i -> v u z k w i", w=N_PAIRS, v=PAIR, u=2, z=2, k=BAND)
        products_of_chunk = []
        dq_tile = const.tile([P, HEADS, ROAD, PACK], BF16, align_bytes=64)
        result_tile = const.tile([P, N_PAIRS, DIM], F32)
        g_il = const.tile([P, HEADS, ROAD, PACK], BF16)
        x_grouped = const.tile([P, DIM, PACK], BF16, align_bytes=64)
        g_cos_feat = const.tile([P, ROAD, HEADS, PACK], F32)
        dq_feat = const.tile([P, 2, N_QUADS, BAND, QUAD, PACK], BF16, align_bytes=64)
        result_feat = const.tile([P, 2, N_QUADS, DIM], F32)

        def words(c):
            first_head, n_heads = CHUNKS[c]
            return g_all[:, :, first_head : first_head + n_heads, :].rearrange("p b h d -> p h d b")

        def products(c):
            n_heads = CHUNKS[c][1]
            table_source = tables if c == 0 else tables_psum
            g_words = words(c)
            g_cos = work.tile([P, MAX_CHUNK, ROAD, PACK], F32)
            g_sin = work.tile([P, MAX_CHUNK, ROAD, PACK], F32)
            for u in range(2):
                band = slice(HALF * u + BAND, HALF * u + 2 * BAND)
                partner = slice(HALF * (1 - u) + BAND, HALF * (1 - u) + 2 * BAND)
                place = slice(BAND * u, BAND * (u + 1))
                nc.vector.tensor_tensor(
                    out=g_cos[:, 0:n_heads, place, :],
                    in0=g_words[:, :, band, :],
                    in1=over_heads_and_batches(table_source[:, 0, band], n_heads),
                    op=MULT,
                )
                nc.vector.tensor_tensor(
                    out=g_sin[:, 0:n_heads, place, :],
                    in0=g_words[:, :, partner, :],
                    in1=over_heads_and_batches(table_source[:, 1, band], n_heads),
                    op=MULT,
                )
            products_of_chunk.append((g_cos, g_sin))

        def add(c):
            first_head, n_heads = CHUNKS[c]
            g_cos, g_sin = products_of_chunk[c]
            engine = nc.vector if c == len(CHUNKS) - 1 else nc.gpsimd
            engine.tensor_tensor(
                out=dq_tile[:, first_head : first_head + n_heads],
                in0=g_cos[:, 0:n_heads],
                in1=g_sin[:, 0:n_heads],
                op=ADD,
            )

        def interleave(c):
            first_head, n_heads = CHUNKS[c]
            g_words = words(c)
            for u in range(2):
                nc.scalar.copy(
                    out=g_il[:, first_head : first_head + n_heads, BAND * u : BAND * (u + 1), :],
                    in_=g_words[:, :, HALF * u : HALF * u + BAND, :],
                )

        def multiply(first_column):
            columns = slice(first_column, first_column + P)
            acc = acc_psum.tile([P, N_MOVING], F32)
            nc.tensor.matmul_mx(
                out=acc[:],
                lhsT=dp_codes[:, columns].bitcast(E5M2_X4),
                lhsT_scale=dp_scales[:, columns],
                rhs=x_codes[:].bitcast(E4M3_X4),
                rhs_scale=x_scales[:],
                start=True,
                stop=True,
            )
            return acc

        acc_of_pair = {}

        def quantise_tile_road(first_pair, n_pairs):
            columns = slice(first_pair * P, (first_pair + n_pairs) * P)
            nc.vector.quantize_mx(
                out=dp_codes[:, columns].bitcast(E5M2_X4),
                scales=dp_scales[:, columns],
                in_=dq_tile[:, first_pair * PAIR : (first_pair + n_pairs) * PAIR].rearrange("p h e b -> p (h e b)"),
            )
            for w in range(first_pair, first_pair + n_pairs):
                acc_of_pair[w] = multiply(w * P)

        def empty_tile_road(first_pair, n_pairs):
            for w in range(first_pair, first_pair + n_pairs):
                nc.scalar.copy(out=result_tile[:, w, :], in_=acc_of_pair[w][:, 0:DIM])
            pairs = slice(first_pair, first_pair + n_pairs)
            for v in range(PAIR):
                for u in range(2):
                    rows = slice(ROAD * v + BAND * u, ROAD * v + BAND * (u + 1))
                    nc.sync.dma_start(out=out_tile[v, u, 1][:, pairs, :], in_=result_tile[rows, pairs, :])

        last = len(CHUNKS) - 1
        products(0)
        interleave(0)
        for c in range(last):
            add(c)
            products(c + 1)
            if c == X_BEHIND:
                nc.scalar.copy(out=x_grouped[:], in_=x_raw[:].rearrange("p b i -> p i b"))
            interleave(c + 1)
        nc.vector.quantize_mx(
            out=x_codes[:, 0:DIM].bitcast(E4M3_X4),
            scales=x_scales[:, 0:DIM],
            in_=x_grouped[:].rearrange("p i b -> p (i b)"),
        )
        quantise_tile_road(0, N_PAIRS // 2)
        add(last)
        quantise_tile_road(N_PAIRS // 2, N_PAIRS // 2)

        for f in range(ROAD):
            d = HALF * (f // BAND) + f % BAND
            nc.scalar.activation(
                out=g_cos_feat[:, f], in_=g_il[:, :, f, :], func=COPY, scale=tables32[:, 0, d : d + 1]
            )
            if f in EMPTY_AT:
                empty_tile_road(EMPTY_AT[f][0], EMPTY_AT[f][1])

        acc_of_window = {}

        def quantise_feat_road(u):
            for a in range(N_QUADS):
                first_column = HEADS * ROAD + (u * N_QUADS + a) * P
                columns = slice(first_column, first_column + P)
                nc.vector.quantize_mx(
                    out=dp_codes[:, columns].bitcast(E5M2_X4),
                    scales=dp_scales[:, columns],
                    in_=dq_feat[:, u, a].rearrange("p m l b -> p (m l b)"),
                )
                acc_of_window[(u, a)] = multiply(first_column)

        def empty_feat_road(u):
            for a in range(N_QUADS):
                nc.scalar.copy(out=result_feat[:, u, a, :], in_=acc_of_window[(u, a)][:, 0:DIM])
            for l in range(QUAD):
                nc.sync.dma_start(out=out_feat[l, u, 0], in_=result_feat[l:P:QUAD, u, :, :])

        for f in range(ROAD):
            d = HALF * (f // BAND) + f % BAND
            nc.vector.scalar_tensor_tensor(
                out=dq_feat[:, f // BAND, :, f % BAND, :, :],
                in0=g_il[:, :, (f + BAND) % ROAD, :].rearrange("p (a l) b -> p a l b", a=N_QUADS),
                scalar=tables32[:, 1, d : d + 1],
                in1=g_cos_feat[:, f].rearrange("p (a l) b -> p a l b", a=N_QUADS),
                op0=MULT,
                op1=ADD,
            )
            if f == BAND - 1 + Q_LAG:
                quantise_feat_road(0)
                empty_feat_road(0)
        quantise_feat_road(1)
        empty_feat_road(1)
